import numpy as np
import ml_dtypes


def mxq(x, axis, fmt="e4m3"):
    dtype, down = {"e4m3": (ml_dtypes.float8_e4m3fn, 7), "e5m2": (ml_dtypes.float8_e5m2, 14)}[fmt]
    v = np.moveaxis(np.asarray(x, np.float32).astype(ml_dtypes.bfloat16).astype(np.float64), axis, -1)
    blocks = v.reshape(v.shape[:-1] + (-1, 32))
    amax = np.abs(blocks).max(-1, keepdims=True)
    byte = np.maximum(np.where(amax > 0, np.frexp(amax)[1] - 1 + 127, 0) - down, 1)
    scale = np.exp2(byte - 127.0)
    codes = (blocks / scale).astype(np.float32).astype(dtype).astype(np.float64)
    return np.moveaxis((codes * scale).reshape(v.shape), -1, axis)


WIDE = False


def mx_kscale(k):
    if not WIDE:
        return np.ones(k)
    levels = np.array([10, -10, 5, -5, 0])
    a = np.random.permutation(np.resize(levels, k // 512 * 4)).reshape(k // 512, 4)
    idx = np.arange(k)
    return np.exp2(a[idx // 512, idx % 128 // 32])


BF16 = ml_dtypes.bfloat16


def bf(x):
    return np.asarray(x, np.float32).astype(BF16)


def f64(x):
    return np.asarray(x).astype(np.float64)


H, A, NS, NE, M = 1024, 1024, 1024, 512, 1024


def setup_inputs():
    s, t = mx_kscale(H), mx_kscale(H)
    wsc = 0.25 / np.sqrt(H)
    return {
        "attendee_stmts": bf(np.random.standard_normal((NS, H)) * s),
        "attendee_eres": bf(np.random.standard_normal((NE, H)) * s),
        "attender": bf(np.random.standard_normal((M, H)) * 0.2 / t),
        "W_ss": bf(np.random.standard_normal((H, H)) * wsc * t[:, None] / s),
        "b_ss": bf(np.random.standard_normal(H) * 0.1 * t),
        "W_es": bf(np.random.standard_normal((H, H)) * wsc * t[:, None] / s),
        "b_es": bf(np.random.standard_normal(H) * 0.1 * t),
    }


def reference(attendee_stmts, attendee_eres, attender, W_ss, b_ss, W_es, b_es):
    aq = mxq(f64(attender), 1, "e4m3")
    p_ss = (mxq(f64(attendee_stmts), 1, "e4m3") @ mxq(f64(W_ss), 1, "e4m3").T) + f64(b_ss)
    p_es = (mxq(f64(attendee_eres), 1, "e4m3") @ mxq(f64(W_es), 1, "e4m3").T) + f64(b_es)
    scores_ss = mxq(p_ss, 1, "e4m3") @ aq.T
    scores_es = mxq(p_es, 1, "e4m3") @ aq.T
    return scores_ss, scores_es

@@ -1,0 +1,183 @@
+from contextlib import ExitStack
+
+import concourse.mybir as mybir
+from concourse.masks import make_identity
+
+F32 = mybir.dt.float32
+BF16 = mybir.dt.bfloat16
+U32 = mybir.dt.uint32
+U8 = mybir.dt.uint8
+FP8X4 = mybir.dt.float8_e4m3fn_x4
+
+P = 128
+H = 1024
+PACK = 4
+PASSES = H // (P * PACK)
+UNITS = 4
+SLAB = UNITS * P
+BANK = 512
+WORDS = H // 2
+M = 1024
+
+FLOPS = 2 * 2 * (1024 + 512) * H * H
+
+
+def unit_cols(j):
+    return slice(j * P, (j + 1) * P)
+
+
+def tile_attention_pa_kernel(
+    tc, attendee_stmts, attendee_eres, attender, W_ss, b_ss, W_es, b_es, out_0, out_1
+):
+    nc = tc.nc
+    with ExitStack() as ctx:
+        consts = ctx.enter_context(tc.tile_pool(name="consts", bufs=1))
+        raws = ctx.enter_context(tc.tile_pool(name="raws", bufs=1))
+        keep = ctx.enter_context(tc.tile_pool(name="keep", bufs=1))
+        stage = ctx.enter_context(tc.tile_pool(name="stage", bufs=6))
+        outs = ctx.enter_context(tc.tile_pool(name="outs", bufs=4))
+        psum = ctx.enter_context(tc.psum_pool(name="psum", bufs=8))
+        ctx.enter_context(tc.manual_schedule())
+
+        def load_slab(name, units):
+            raw = raws.tile([P, UNITS * H], BF16, name=name)
+            for j in range(UNITS):
+                nc.sync.dma_start(out=raw[:, j * H : (j + 1) * H], in_=units[j])
+            return raw
+
+        def plain_units(matrix, slab):
+            view = matrix.rearrange("(c j r) h -> c j r h", j=UNITS, r=P)
+            return [view[slab, j] for j in range(UNITS)]
+
+        def paired_units(weight, slab):
+            view = weight.rearrange("(c u r e) h -> c u e r h", u=2, r=P, e=2)
+            return [view[slab, t // 2, t % 2] for t in range(UNITS)]
+
+        raw_w_es = [load_slab("raw_w_es0", paired_units(W_es, 0))]
+        raw_x_es = load_slab("raw_x_es", plain_units(attendee_eres, 0))
+        raw_w_es.append(load_slab("raw_w_es1", paired_units(W_es, 1)))
+        raw_a = [load_slab("raw_a%d" % c, plain_units(attender, c)) for c in range(2)]
+        raw_w_ss = [load_slab("raw_w_ss0", paired_units(W_ss, 0))]
+        raw_x_ss = [load_slab("raw_x_ss0", plain_units(attendee_stmts, 0))]
+        raw_w_ss.append(load_slab("raw_w_ss1", paired_units(W_ss, 1)))
+        raw_x_ss.append(load_slab("raw_x_ss1", plain_units(attendee_stmts, 1)))
+
+        ident = consts.tile([P, P], F32, name="ident")
+        make_identity(nc, ident[:])
+
+        bias_rows = consts.tile([P, 2 * P], BF16, name="bias_rows")
+        nc.vector.memset(bias_rows[:], 0.0)
+        nc.scalar.dma_start(out=bias_rows[0:4, :], in_=b_ss.rearrange("(c w) -> c w", w=2 * P))
+        nc.scalar.dma_start(out=bias_rows[4:8, :], in_=b_es.rearrange("(c w) -> c w", w=2 * P))
+
+        def new_bank():
+            bank = psum.tile([P, BANK], F32, name="bank", tag="bank")
+            return bank
+
+        def spread_biases():
+            bank = new_bank()
+            nc.tensor.transpose(bank[:, 0:P], bias_rows[:].bitcast(F32), ident[:])
+            bias_pairs = consts.tile([P, 16], BF16, name="bias_pairs")
+            nc.vector.tensor_copy(out=bias_pairs[:].bitcast(F32), in_=bank[:, 0:8])
+            bias = consts.tile([P, 16], F32, name="bias")
+            nc.vector.tensor_copy(out=bias[:], in_=bias_pairs[:])
+            return bias
+
+        def new_operand(name):
+            codes = keep.tile([P, PASSES, SLAB], U32, name="%s_codes" % name, align_bytes=64)
+            scales = keep.tile([P, PASSES, SLAB], U8, name="%s_scales" % name, align_bytes=64)
+            return codes, scales
+
+        def quantise(grouped, operand, g, cols):
+            codes, scales = operand
+            nc.vector.quantize_mx(
+                out=codes[:, g, cols].bitcast(FP8X4), scales=scales[:, g, cols], in_=grouped
+            )
+
+        def transpose_slab(raw, name):
+            operand = new_operand(name)
+            raw_words = raw[:].bitcast(F32)
+            for j in range(UNITS):
+                bank = new_bank()
+                for c in range(WORDS // P):
+                    nc.tensor.transpose(
+                        bank[:, unit_cols(c)],
+                        raw_words[:, j * WORDS + c * P : j * WORDS + (c + 1) * P],
+                        ident[:],
+                    )
+                grouped = stage.tile([P, PASSES * P * PACK], BF16, name="grouped", align_bytes=64)
+                nc.scalar.copy(
+                    out=grouped[:].bitcast(F32).rearrange("p (g r u) -> p g r u", g=PASSES, u=2),
+                    in_=bank[:].rearrange("p (g u r) -> p g r u", g=PASSES, u=2),
+                )
+                for g in range(PASSES):
+                    quantise(grouped[:, g * P * PACK : (g + 1) * P * PACK], operand, g, unit_cols(j))
+            return operand
+
+        def mx_group(out, stationary, stationary_cols, moving, moving_cols):
+            for g in range(PASSES):
+                nc.tensor.matmul_mx(
+                    out=out,
+                    lhsT=stationary[0][:, g, stationary_cols].bitcast(FP8X4),
+                    lhsT_scale=stationary[1][:, g, stationary_cols],
+                    rhs=moving[0][:, g, moving_cols].bitcast(FP8X4),
+                    rhs_scale=moving[1][:, g, moving_cols],
+                    start=(g == 0),
+                    stop=(g == PASSES - 1),
+                )
+
+        def stage1(x, w, bias_cols, p, g2):
+            grouped_units = []
+            for j in range(UNITS):
+                bank = new_bank()
+                for t in range(PACK):
+                    mx_group(bank[:, unit_cols(t)], w, unit_cols(t), x, unit_cols(j))
+                p_grouped = stage.tile([P, P, PACK], BF16, name="p_grouped", align_bytes=64)
+                nc.vector.tensor_tensor(
+                    out=p_grouped[:],
+                    in0=bank[:].rearrange("p (t s) -> p s t", t=PACK),
+                    in1=bias_cols.unsqueeze(1).to_broadcast([P, P, PACK]),
+                    op=mybir.AluOpType.add,
+                )
+                grouped_units.append(p_grouped[:].rearrange("p s t -> p (s t)"))
+                if j > 0:
+                    quantise(grouped_units[j - 1], p, g2, unit_cols(j - 1))
+            quantise(grouped_units[UNITS - 1], p, g2, unit_cols(UNITS - 1))
+
+        def stage2(p, a, out_units, units):
+            for j in units:
+                scores = outs.tile([P, M], F32, name="scores")
+                for c in range(M // BANK):
+                    bank = new_bank()
+                    mx_group(bank[:], p, unit_cols(j), a[c], slice(0, SLAB))
+                    nc.scalar.copy(out=scores[:, c * BANK : (c + 1) * BANK], in_=bank[:])
+                nc.sync.dma_start(out=out_units[j], in_=scores[:])
+
+        out_es = out_1.rearrange("(c j r) m -> c j r m", j=UNITS, r=P)
+        out_ss = out_0.rearrange("(c j r) m -> c j r m", j=UNITS, r=P)
+        p_es = new_operand("p_es")
+        p_ss = [new_operand("p_ss%d" % c) for c in range(2)]
+
+        w_es = [transpose_slab(raw_w_es[0], "w_es0")]
+        bias = spread_biases()
+        bias_ss = [bias[:, 4 * g2 : 4 * g2 + 4] for g2 in range(PASSES)]
+        bias_es = [bias[:, 8 + 4 * g2 : 8 + 4 * g2 + 4] for g2 in range(PASSES)]
+        x_es = transpose_slab(raw_x_es, "x_es")
+        stage1(x_es, w_es[0], bias_es[0], p_es, 0)
+        w_es.append(transpose_slab(raw_w_es[1], "w_es1"))
+        a = [transpose_slab(raw_a[0], "a0")]
+        stage1(x_es, w_es[1], bias_es[1], p_es, 1)
+        a.append(transpose_slab(raw_a[1], "a1"))
+        w_ss = [transpose_slab(raw_w_ss[0], "w_ss0")]
+        stage2(p_es, a, out_es[0], [0, 1])
+        x_ss = [transpose_slab(raw_x_ss[0], "x_ss0")]
+        stage2(p_es, a, out_es[0], [2, 3])
+        w_ss.append(transpose_slab(raw_w_ss[1], "w_ss1"))
+        stage1(x_ss[0], w_ss[0], bias_ss[0], p_ss[0], 0)
+        x_ss.append(transpose_slab(raw_x_ss[1], "x_ss1"))
+        stage1(x_ss[0], w_ss[1], bias_ss[1], p_ss[0], 1)
+        stage1(x_ss[1], w_ss[0], bias_ss[0], p_ss[1], 0)
+        stage2(p_ss[0], a, out_ss[0], [0, 1])
+        stage1(x_ss[1], w_ss[1], bias_ss[1], p_ss[1], 1)
+        stage2(p_ss[0], a, out_ss[0], [2, 3])
+        stage2(p_ss[1], a, out_ss[1], [0, 1, 2, 3])

@@ -53,14 +53,15 @@ def tile_attention_pa_kernel(
             view = weight.rearrange("(c u r e) h -> c u e r h", u=2, r=P, e=2)
             return [view[slab, t // 2, t % 2] for t in range(UNITS)]
 
-        raw_w_es = [load_slab("raw_w_es0", paired_units(W_es, 0))]
-        raw_x_es = load_slab("raw_x_es", plain_units(attendee_eres, 0))
-        raw_w_es.append(load_slab("raw_w_es1", paired_units(W_es, 1)))
-        raw_a = [load_slab("raw_a%d" % c, plain_units(attender, c)) for c in range(2)]
         raw_w_ss = [load_slab("raw_w_ss0", paired_units(W_ss, 0))]
         raw_x_ss = [load_slab("raw_x_ss0", plain_units(attendee_stmts, 0))]
         raw_w_ss.append(load_slab("raw_w_ss1", paired_units(W_ss, 1)))
+        raw_a = [load_slab("raw_a0", plain_units(attender, 0))]
         raw_x_ss.append(load_slab("raw_x_ss1", plain_units(attendee_stmts, 1)))
+        raw_a.append(load_slab("raw_a1", plain_units(attender, 1)))
+        raw_w_es = [load_slab("raw_w_es0", paired_units(W_es, 0))]
+        raw_x_es = load_slab("raw_x_es", plain_units(attendee_eres, 0))
+        raw_w_es.append(load_slab("raw_w_es1", paired_units(W_es, 1)))
 
         ident = consts.tile([P, P], F32, name="ident")
         make_identity(nc, ident[:])
@@ -150,7 +151,10 @@ def tile_attention_pa_kernel(
                 for c in range(M // BANK):
                     bank = new_bank()
                     mx_group(bank[:], p, unit_cols(j), a[c], slice(0, SLAB))
-                    nc.scalar.copy(out=scores[:, c * BANK : (c + 1) * BANK], in_=bank[:])
+                    if c == 0:
+                        nc.scalar.copy(out=scores[:, c * BANK : (c + 1) * BANK], in_=bank[:])
+                    else:
+                        nc.vector.tensor_copy(out=scores[:, c * BANK : (c + 1) * BANK], in_=bank[:])
                 nc.sync.dma_start(out=out_units[j], in_=scores[:])
 
         out_es = out_1.rearrange("(c j r) m -> c j r m", j=UNITS, r=P)
@@ -158,26 +162,26 @@ def tile_attention_pa_kernel(
         p_es = new_operand("p_es")
         p_ss = [new_operand("p_ss%d" % c) for c in range(2)]
 
-        w_es = [transpose_slab(raw_w_es[0], "w_es0")]
+        w_ss = [transpose_slab(raw_w_ss[0], "w_ss0")]
         bias = spread_biases()
         bias_ss = [bias[:, 4 * g2 : 4 * g2 + 4] for g2 in range(PASSES)]
         bias_es = [bias[:, 8 + 4 * g2 : 8 + 4 * g2 + 4] for g2 in range(PASSES)]
-        x_es = transpose_slab(raw_x_es, "x_es")
-        stage1(x_es, w_es[0], bias_es[0], p_es, 0)
-        w_es.append(transpose_slab(raw_w_es[1], "w_es1"))
-        a = [transpose_slab(raw_a[0], "a0")]
-        stage1(x_es, w_es[1], bias_es[1], p_es, 1)
-        a.append(transpose_slab(raw_a[1], "a1"))
-        w_ss = [transpose_slab(raw_w_ss[0], "w_ss0")]
-        stage2(p_es, a, out_es[0], [0, 1])
         x_ss = [transpose_slab(raw_x_ss[0], "x_ss0")]
-        stage2(p_es, a, out_es[0], [2, 3])
-        w_ss.append(transpose_slab(raw_w_ss[1], "w_ss1"))
         stage1(x_ss[0], w_ss[0], bias_ss[0], p_ss[0], 0)
-        x_ss.append(transpose_slab(raw_x_ss[1], "x_ss1"))
+        w_ss.append(transpose_slab(raw_w_ss[1], "w_ss1"))
+        a = [transpose_slab(raw_a[0], "a0")]
         stage1(x_ss[0], w_ss[1], bias_ss[1], p_ss[0], 1)
+        x_ss.append(transpose_slab(raw_x_ss[1], "x_ss1"))
+        a.append(transpose_slab(raw_a[1], "a1"))
         stage1(x_ss[1], w_ss[0], bias_ss[0], p_ss[1], 0)
         stage2(p_ss[0], a, out_ss[0], [0, 1])
+        w_es = [transpose_slab(raw_w_es[0], "w_es0")]
         stage1(x_ss[1], w_ss[1], bias_ss[1], p_ss[1], 1)
         stage2(p_ss[0], a, out_ss[0], [2, 3])
-        stage2(p_ss[1], a, out_ss[1], [0, 1, 2, 3])
+        x_es = transpose_slab(raw_x_es, "x_es")
+        stage2(p_ss[1], a, out_ss[1], [0, 1])
+        w_es.append(transpose_slab(raw_w_es[1], "w_es1"))
+        stage1(x_es, w_es[0], bias_es[0], p_es, 0)
+        stage1(x_es, w_es[1], bias_es[1], p_es, 1)
+        stage2(p_ss[1], a, out_ss[1], [2, 3])
+        stage2(p_es, a, out_es[0], [0, 1, 2, 3])

@@ -35,7 +35,7 @@ def tile_attention_pa_kernel(
         raws = ctx.enter_context(tc.tile_pool(name="raws", bufs=1))
         keep = ctx.enter_context(tc.tile_pool(name="keep", bufs=1))
         stage = ctx.enter_context(tc.tile_pool(name="stage", bufs=6))
-        outs = ctx.enter_context(tc.tile_pool(name="outs", bufs=4))
+        outs = ctx.enter_context(tc.tile_pool(name="outs", bufs=8))
         psum = ctx.enter_context(tc.psum_pool(name="psum", bufs=8))
         ctx.enter_context(tc.manual_schedule())
 
@@ -53,15 +53,14 @@ def tile_attention_pa_kernel(
             view = weight.rearrange("(c u r e) h -> c u e r h", u=2, r=P, e=2)
             return [view[slab, t // 2, t % 2] for t in range(UNITS)]
 
-        raw_w_ss = [load_slab("raw_w_ss0", paired_units(W_ss, 0))]
-        raw_x_ss = [load_slab("raw_x_ss0", plain_units(attendee_stmts, 0))]
-        raw_w_ss.append(load_slab("raw_w_ss1", paired_units(W_ss, 1)))
-        raw_a = [load_slab("raw_a0", plain_units(attender, 0))]
-        raw_x_ss.append(load_slab("raw_x_ss1", plain_units(attendee_stmts, 1)))
-        raw_a.append(load_slab("raw_a1", plain_units(attender, 1)))
         raw_w_es = [load_slab("raw_w_es0", paired_units(W_es, 0))]
         raw_x_es = load_slab("raw_x_es", plain_units(attendee_eres, 0))
         raw_w_es.append(load_slab("raw_w_es1", paired_units(W_es, 1)))
+        raw_a = [load_slab("raw_a%d" % c, plain_units(attender, c)) for c in range(2)]
+        raw_w_ss = [load_slab("raw_w_ss0", paired_units(W_ss, 0))]
+        raw_x_ss = [load_slab("raw_x_ss0", plain_units(attendee_stmts, 0))]
+        raw_w_ss.append(load_slab("raw_w_ss1", paired_units(W_ss, 1)))
+        raw_x_ss.append(load_slab("raw_x_ss1", plain_units(attendee_stmts, 1)))
 
         ident = consts.tile([P, P], F32, name="ident")
         make_identity(nc, ident[:])
@@ -127,9 +126,9 @@ def tile_attention_pa_kernel(
                     stop=(g == PASSES - 1),
                 )
 
-        def stage1(x, w, bias_cols, p, g2):
-            grouped_units = []
-            for j in range(UNITS):
+        def stage1(x, w, bias_cols, p, g2, units):
+            waiting = None
+            for j in units:
                 bank = new_bank()
                 for t in range(PACK):
                     mx_group(bank[:, unit_cols(t)], w, unit_cols(t), x, unit_cols(j))
@@ -140,21 +139,21 @@ def tile_attention_pa_kernel(
                     in1=bias_cols.unsqueeze(1).to_broadcast([P, P, PACK]),
                     op=mybir.AluOpType.add,
                 )
-                grouped_units.append(p_grouped[:].rearrange("p s t -> p (s t)"))
-                if j > 0:
-                    quantise(grouped_units[j - 1], p, g2, unit_cols(j - 1))
-            quantise(grouped_units[UNITS - 1], p, g2, unit_cols(UNITS - 1))
+                if waiting is not None:
+                    quantise(waiting[0], p, g2, unit_cols(waiting[1]))
+                waiting = (p_grouped[:].rearrange("p s t -> p (s t)"), j)
+            quantise(waiting[0], p, g2, unit_cols(waiting[1]))
 
-        def stage2(p, a, out_units, units):
+        def stage2(p, a, out_units, units, vector_helps):
             for j in units:
                 scores = outs.tile([P, M], F32, name="scores")
                 for c in range(M // BANK):
                     bank = new_bank()
                     mx_group(bank[:], p, unit_cols(j), a[c], slice(0, SLAB))
-                    if c == 0:
-                        nc.scalar.copy(out=scores[:, c * BANK : (c + 1) * BANK], in_=bank[:])
-                    else:
+                    if vector_helps and c == 1:
                         nc.vector.tensor_copy(out=scores[:, c * BANK : (c + 1) * BANK], in_=bank[:])
+                    else:
+                        nc.scalar.copy(out=scores[:, c * BANK : (c + 1) * BANK], in_=bank[:])
                 nc.sync.dma_start(out=out_units[j], in_=scores[:])
 
         out_es = out_1.rearrange("(c j r) m -> c j r m", j=UNITS, r=P)
@@ -162,26 +161,29 @@ def tile_attention_pa_kernel(
         p_es = new_operand("p_es")
         p_ss = [new_operand("p_ss%d" % c) for c in range(2)]
 
-        w_ss = [transpose_slab(raw_w_ss[0], "w_ss0")]
+        first, second, whole = [0, 1], [2, 3], [0, 1, 2, 3]
+        w_es = [transpose_slab(raw_w_es[0], "w_es0")]
         bias = spread_biases()
         bias_ss = [bias[:, 4 * g2 : 4 * g2 + 4] for g2 in range(PASSES)]
         bias_es = [bias[:, 8 + 4 * g2 : 8 + 4 * g2 + 4] for g2 in range(PASSES)]
-        x_ss = [transpose_slab(raw_x_ss[0], "x_ss0")]
-        stage1(x_ss[0], w_ss[0], bias_ss[0], p_ss[0], 0)
-        w_ss.append(transpose_slab(raw_w_ss[1], "w_ss1"))
-        a = [transpose_slab(raw_a[0], "a0")]
-        stage1(x_ss[0], w_ss[1], bias_ss[1], p_ss[0], 1)
-        x_ss.append(transpose_slab(raw_x_ss[1], "x_ss1"))
-        a.append(transpose_slab(raw_a[1], "a1"))
-        stage1(x_ss[1], w_ss[0], bias_ss[0], p_ss[1], 0)
-        stage2(p_ss[0], a, out_ss[0], [0, 1])
-        w_es = [transpose_slab(raw_w_es[0], "w_es0")]
-        stage1(x_ss[1], w_ss[1], bias_ss[1], p_ss[1], 1)
-        stage2(p_ss[0], a, out_ss[0], [2, 3])
         x_es = transpose_slab(raw_x_es, "x_es")
-        stage2(p_ss[1], a, out_ss[1], [0, 1])
+        stage1(x_es, w_es[0], bias_es[0], p_es, 0, first)
         w_es.append(transpose_slab(raw_w_es[1], "w_es1"))
-        stage1(x_es, w_es[0], bias_es[0], p_es, 0)
-        stage1(x_es, w_es[1], bias_es[1], p_es, 1)
-        stage2(p_ss[1], a, out_ss[1], [2, 3])
-        stage2(p_es, a, out_es[0], [0, 1, 2, 3])
+        stage1(x_es, w_es[0], bias_es[0], p_es, 0, second)
+        a = [transpose_slab(raw_a[0], "a0")]
+        stage1(x_es, w_es[1], bias_es[1], p_es, 1, first)
+        a.append(transpose_slab(raw_a[1], "a1"))
+        stage1(x_es, w_es[1], bias_es[1], p_es, 1, second)
+        w_ss = [transpose_slab(raw_w_ss[0], "w_ss0")]
+        stage2(p_es, a, out_es[0], first, True)
+        x_ss = [transpose_slab(raw_x_ss[0], "x_ss0")]
+        stage2(p_es, a, out_es[0], second, True)
+        w_ss.append(transpose_slab(raw_w_ss[1], "w_ss1"))
+        stage1(x_ss[0], w_ss[0], bias_ss[0], p_ss[0], 0, whole)
+        x_ss.append(transpose_slab(raw_x_ss[1], "x_ss1"))
+        stage1(x_ss[0], w_ss[1], bias_ss[1], p_ss[0], 1, whole)
+        stage1(x_ss[1], w_ss[0], bias_ss[0], p_ss[1], 0, whole)
+        stage2(p_ss[0], a, out_ss[0], first, False)
+        stage1(x_ss[1], w_ss[1], bias_ss[1], p_ss[1], 1, whole)
+        stage2(p_ss[0], a, out_ss[0], second, False)
+        stage2(p_ss[1], a, out_ss[1], whole, False)

from contextlib import ExitStack

import concourse.mybir as mybir
from concourse.masks import make_identity

F32 = mybir.dt.float32
BF16 = mybir.dt.bfloat16
U32 = mybir.dt.uint32
U8 = mybir.dt.uint8
FP8X4 = mybir.dt.float8_e4m3fn_x4

P = 128
H = 1024
PACK = 4
PASSES = H // (P * PACK)
UNITS = 4
SLAB = UNITS * P
BANK = 512
WORDS = H // 2
M = 1024

FLOPS = 2 * 2 * (1024 + 512) * H * H


def unit_cols(j):
    return slice(j * P, (j + 1) * P)


def tile_attention_pa_kernel(
    tc, attendee_stmts, attendee_eres, attender, W_ss, b_ss, W_es, b_es, out_0, out_1
):
    nc = tc.nc
    with ExitStack() as ctx:
        consts = ctx.enter_context(tc.tile_pool(name="consts", bufs=1))
        raws = ctx.enter_context(tc.tile_pool(name="raws", bufs=1))
        keep = ctx.enter_context(tc.tile_pool(name="keep", bufs=1))
        stage = ctx.enter_context(tc.tile_pool(name="stage", bufs=6))
        outs = ctx.enter_context(tc.tile_pool(name="outs", bufs=8))
        psum = ctx.enter_context(tc.psum_pool(name="psum", bufs=8))
        ctx.enter_context(tc.manual_schedule())

        def load_slab(name, units):
            raw = raws.tile([P, UNITS * H], BF16, name=name)
            for j in range(UNITS):
                nc.sync.dma_start(out=raw[:, j * H : (j + 1) * H], in_=units[j])
            return raw

        def plain_units(matrix, slab):
            view = matrix.rearrange("(c j r) h -> c j r h", j=UNITS, r=P)
            return [view[slab, j] for j in range(UNITS)]

        def paired_units(weight, slab):
            view = weight.rearrange("(c u r e) h -> c u e r h", u=2, r=P, e=2)
            return [view[slab, t // 2, t % 2] for t in range(UNITS)]

        raw_w_es = [load_slab("raw_w_es0", paired_units(W_es, 0))]
        raw_x_es = load_slab("raw_x_es", plain_units(attendee_eres, 0))
        raw_w_es.append(load_slab("raw_w_es1", paired_units(W_es, 1)))
        raw_a = [load_slab("raw_a%d" % c, plain_units(attender, c)) for c in range(2)]
        raw_w_ss = [load_slab("raw_w_ss0", paired_units(W_ss, 0))]
        raw_x_ss = [load_slab("raw_x_ss0", plain_units(attendee_stmts, 0))]
        raw_w_ss.append(load_slab("raw_w_ss1", paired_units(W_ss, 1)))
        raw_x_ss.append(load_slab("raw_x_ss1", plain_units(attendee_stmts, 1)))

        ident = consts.tile([P, P], F32, name="ident")
        make_identity(nc, ident[:])

        bias_rows = consts.tile([P, 2 * P], BF16, name="bias_rows")
        nc.vector.memset(bias_rows[:], 0.0)
        nc.scalar.dma_start(out=bias_rows[0:4, :], in_=b_ss.rearrange("(c w) -> c w", w=2 * P))
        nc.scalar.dma_start(out=bias_rows[4:8, :], in_=b_es.rearrange("(c w) -> c w", w=2 * P))

        def new_bank():
            bank = psum.tile([P, BANK], F32, name="bank", tag="bank")
            return bank

        def spread_biases():
            bank = new_bank()
            nc.tensor.transpose(bank[:, 0:P], bias_rows[:].bitcast(F32), ident[:])
            bias_pairs = consts.tile([P, 16], BF16, name="bias_pairs")
            nc.vector.tensor_copy(out=bias_pairs[:].bitcast(F32), in_=bank[:, 0:8])
            bias = consts.tile([P, 16], F32, name="bias")
            nc.vector.tensor_copy(out=bias[:], in_=bias_pairs[:])
            return bias

        def new_operand(name):
            codes = keep.tile([P, PASSES, SLAB], U32, name="%s_codes" % name, align_bytes=64)
            scales = keep.tile([P, PASSES, SLAB], U8, name="%s_scales" % name, align_bytes=64)
            return codes, scales

        def quantise(grouped, operand, g, cols):
            codes, scales = operand
            nc.vector.quantize_mx(
                out=codes[:, g, cols].bitcast(FP8X4), scales=scales[:, g, cols], in_=grouped
            )

        def transpose_slab(raw, name):
            operand = new_operand(name)
            raw_words = raw[:].bitcast(F32)
            for j in range(UNITS):
                bank = new_bank()
                for c in range(WORDS // P):
                    nc.tensor.transpose(
                        bank[:, unit_cols(c)],
                        raw_words[:, j * WORDS + c * P : j * WORDS + (c + 1) * P],
                        ident[:],
                    )
                grouped = stage.tile([P, PASSES * P * PACK], BF16, name="grouped", align_bytes=64)
                nc.scalar.copy(
                    out=grouped[:].bitcast(F32).rearrange("p (g r u) -> p g r u", g=PASSES, u=2),
                    in_=bank[:].rearrange("p (g u r) -> p g r u", g=PASSES, u=2),
                )
                for g in range(PASSES):
                    quantise(grouped[:, g * P * PACK : (g + 1) * P * PACK], operand, g, unit_cols(j))
            return operand

        def mx_group(out, stationary, stationary_cols, moving, moving_cols):
            for g in range(PASSES):
                nc.tensor.matmul_mx(
                    out=out,
                    lhsT=stationary[0][:, g, stationary_cols].bitcast(FP8X4),
                    lhsT_scale=stationary[1][:, g, stationary_cols],
                    rhs=moving[0][:, g, moving_cols].bitcast(FP8X4),
                    rhs_scale=moving[1][:, g, moving_cols],
                    start=(g == 0),
                    stop=(g == PASSES - 1),
                )

        def stage1(x, w, bias_cols, p, g2, units):
            waiting = None
            for j in units:
                bank = new_bank()
                for t in range(PACK):
                    mx_group(bank[:, unit_cols(t)], w, unit_cols(t), x, unit_cols(j))
                p_grouped = stage.tile([P, P, PACK], BF16, name="p_grouped", align_bytes=64)
                nc.vector.tensor_tensor(
                    out=p_grouped[:],
                    in0=bank[:].rearrange("p (t s) -> p s t", t=PACK),
                    in1=bias_cols.unsqueeze(1).to_broadcast([P, P, PACK]),
                    op=mybir.AluOpType.add,
                )
                if waiting is not None:
                    quantise(waiting[0], p, g2, unit_cols(waiting[1]))
                waiting = (p_grouped[:].rearrange("p s t -> p (s t)"), j)
            quantise(waiting[0], p, g2, unit_cols(waiting[1]))

        def stage2(p, a, out_units, units, vector_helps):
            for j in units:
                scores = outs.tile([P, M], F32, name="scores")
                for c in range(M // BANK):
                    bank = new_bank()
                    mx_group(bank[:], p, unit_cols(j), a[c], slice(0, SLAB))
                    if vector_helps and c == 1:
                        nc.vector.tensor_copy(out=scores[:, c * BANK : (c + 1) * BANK], in_=bank[:])
                    else:
                        nc.scalar.copy(out=scores[:, c * BANK : (c + 1) * BANK], in_=bank[:])
                nc.sync.dma_start(out=out_units[j], in_=scores[:])

        out_es = out_1.rearrange("(c j r) m -> c j r m", j=UNITS, r=P)
        out_ss = out_0.rearrange("(c j r) m -> c j r m", j=UNITS, r=P)
        p_es = new_operand("p_es")
        p_ss = [new_operand("p_ss%d" % c) for c in range(2)]

        first, second, whole = [0, 1], [2, 3], [0, 1, 2, 3]
        w_es = [transpose_slab(raw_w_es[0], "w_es0")]
        bias = spread_biases()
        bias_ss = [bias[:, 4 * g2 : 4 * g2 + 4] for g2 in range(PASSES)]
        bias_es = [bias[:, 8 + 4 * g2 : 8 + 4 * g2 + 4] for g2 in range(PASSES)]
        x_es = transpose_slab(raw_x_es, "x_es")
        stage1(x_es, w_es[0], bias_es[0], p_es, 0, first)
        w_es.append(transpose_slab(raw_w_es[1], "w_es1"))
        stage1(x_es, w_es[0], bias_es[0], p_es, 0, second)
        a = [transpose_slab(raw_a[0], "a0")]
        stage1(x_es, w_es[1], bias_es[1], p_es, 1, first)
        a.append(transpose_slab(raw_a[1], "a1"))
        stage1(x_es, w_es[1], bias_es[1], p_es, 1, second)
        w_ss = [transpose_slab(raw_w_ss[0], "w_ss0")]
        stage2(p_es, a, out_es[0], first, True)
        x_ss = [transpose_slab(raw_x_ss[0], "x_ss0")]
        stage2(p_es, a, out_es[0], second, True)
        w_ss.append(transpose_slab(raw_w_ss[1], "w_ss1"))
        stage1(x_ss[0], w_ss[0], bias_ss[0], p_ss[0], 0, whole)
        x_ss.append(transpose_slab(raw_x_ss[1], "x_ss1"))
        stage1(x_ss[0], w_ss[1], bias_ss[1], p_ss[0], 1, whole)
        stage1(x_ss[1], w_ss[0], bias_ss[0], p_ss[1], 0, whole)
        stage2(p_ss[0], a, out_ss[0], first, False)
        stage1(x_ss[1], w_ss[1], bias_ss[1], p_ss[1], 1, whole)
        stage2(p_ss[0], a, out_ss[0], second, False)
        stage2(p_ss[1], a, out_ss[1], whole, False)
